import numpy as np
import ml_dtypes


def mxq(x, axis, fmt="e4m3"):
    dtype, down = {"e4m3": (ml_dtypes.float8_e4m3fn, 7), "e5m2": (ml_dtypes.float8_e5m2, 14)}[fmt]
    v = np.moveaxis(np.asarray(x, np.float32).astype(ml_dtypes.bfloat16).astype(np.float64), axis, -1)
    blocks = v.reshape(v.shape[:-1] + (-1, 32))
    amax = np.abs(blocks).max(-1, keepdims=True)
    byte = np.maximum(np.where(amax > 0, np.frexp(amax)[1] - 1 + 127, 0) - down, 1)
    scale = np.exp2(byte - 127.0)
    codes = (blocks / scale).astype(np.float32).astype(dtype).astype(np.float64)
    return np.moveaxis((codes * scale).reshape(v.shape), -1, axis)


WIDE = False


def mx_kscale(k):
    if not WIDE:
        return np.ones(k)
    levels = np.array([10, -10, 5, -5, 0])
    a = np.random.permutation(np.resize(levels, k // 512 * 4)).reshape(k // 512, 4)
    idx = np.arange(k)
    return np.exp2(a[idx // 512, idx % 128 // 32])


BF16 = ml_dtypes.bfloat16


def bf(x):
    return np.asarray(x, np.float32).astype(BF16)


def f64(x):
    return np.asarray(x).astype(np.float64)


E2M1 = np.array([0.0, 0.5, 1.0, 1.5, 2.0, 3.0, 4.0, 6.0, -0.0, -0.5, -1.0, -1.5, -2.0, -3.0, -4.0, -6.0])


def pack_weight(w, fmt):
    k, n = w.shape
    w = f64(bf(w)).reshape(k // 32, 32, n)
    amax = np.abs(w).max(1)
    if fmt == "e4m3":
        byte = np.frexp(amax)[1] - 1 + 127 - 7
    else:
        mant, ex = np.frexp(amax / 6.0)
        byte = np.where(mant > 0.5, ex, ex - 1) + 127
    byte = np.clip(np.where(amax > 0, byte, 1), 1, 254)
    scaled = (w * np.exp2(127.0 - byte)[:, None, :]).reshape(k, n).astype(np.float32)
    by_word = np.ascontiguousarray(scaled.reshape(k // 512, 128, 4, n).transpose(0, 1, 3, 2))
    if fmt == "e4m3":
        words = by_word.astype(ml_dtypes.float8_e4m3fn).view(np.uint8)
    else:
        c = by_word.astype(ml_dtypes.float4_e2m1fn).view(np.uint8) & 0xF
        words = c[..., 0::2] | (c[..., 1::2] << 4)
    return np.ascontiguousarray(words), np.ascontiguousarray(byte.astype(np.uint8).reshape(k // 512, 16, n))


def unpack_weight(words, scales, fmt):
    g, p, n, _ = words.shape
    if fmt == "e4m3":
        vals = np.ascontiguousarray(words).view(ml_dtypes.float8_e4m3fn).astype(np.float64)
    else:
        nib = np.empty((g, p, n, 4), np.uint8)
        nib[..., 0::2] = words & 0xF
        nib[..., 1::2] = words >> 4
        vals = E2M1[nib]
    vals = vals * np.repeat(np.exp2(scales.astype(np.float64) - 127.0), 8, axis=1)[..., None]
    return vals.transpose(0, 1, 3, 2).reshape(g * 512, n)


B, H, W, C, HIDDEN = 2, 8, 8, 2048, 2048
FMT = "e4m3"


def _perceive(x):
    r = lambda di, dj: np.roll(x, shift=(-di, -dj), axis=(1, 2))
    sx = (r(-1, 1) - r(-1, -1)) + 2.0 * (r(0, 1) - r(0, -1)) + (r(1, 1) - r(1, -1))
    sy = (r(1, -1) - r(-1, -1)) + 2.0 * (r(1, 0) - r(-1, 0)) + (r(1, 1) - r(-1, 1))
    return np.concatenate([sx, sy, x], axis=-1)


def setup_inputs():
    s = mx_kscale(C)
    s3 = np.tile(s, 3)
    t = mx_kscale(HIDDEN)
    state_grid = bf(np.random.standard_normal((B, H, W, C)) * s)
    w_hidden = np.random.standard_normal((HIDDEN, 3 * C)) * 0.6 / np.sqrt(3 * C) / s3[None, :] * t[:, None]
    w_out = np.random.standard_normal((C, HIDDEN)) / np.sqrt(HIDDEN) / t[None, :]
    wh_words, wh_scales = pack_weight(np.ascontiguousarray(w_hidden.T), FMT)
    wo_words, wo_scales = pack_weight(np.ascontiguousarray(w_out.T), FMT)
    return {"state_grid": state_grid,
            "W_hidden_words": wh_words, "W_hidden_scales": wh_scales,
            "W_out_words": wo_words, "W_out_scales": wo_scales}


def reference(state_grid, W_hidden_words, W_hidden_scales, W_out_words, W_out_scales):
    perception = _perceive(f64(state_grid))
    hidden = np.maximum(mxq(perception, 3, "e4m3") @ unpack_weight(W_hidden_words, W_hidden_scales, FMT), 0.0)
    delta_s = mxq(hidden, 3, "e4m3") @ unpack_weight(W_out_words, W_out_scales, FMT)
    return delta_s

@@ -1,0 +1,177 @@
+from contextlib import ExitStack
+
+import concourse.masks as masks
+import concourse.mybir as mybir
+
+F32 = mybir.dt.float32
+BF16 = mybir.dt.bfloat16
+I32 = mybir.dt.int32
+U32 = mybir.dt.uint32
+U8 = mybir.dt.uint8
+FP8X4 = mybir.dt.float8_e4m3fn_x4
+ALU = mybir.AluOpType
+ACT = mybir.ActivationFunctionType
+
+P = 128
+C = 2048
+HIDDEN = 2048
+NCH = 512
+FLOPS = 2 * P * (3 * C) * HIDDEN + 2 * P * HIDDEN * C
+
+
+def tile_nn_w_kernel(tc, state_grid, W_hidden_words, W_hidden_scales, W_out_words, W_out_scales, out):
+    nc = tc.nc
+    x_dram = state_grid.flatten_outer_dims()
+    out_dram = out.flatten_outer_dims()
+    with ExitStack() as ctx:
+        keep = ctx.enter_context(tc.tile_pool(name="keep", bufs=1))
+        tp = ctx.enter_context(tc.psum_pool(name="tp", bufs=4))
+        accp = ctx.enter_context(tc.psum_pool(name="accp", bufs=4))
+        ctx.enter_context(tc.manual_schedule())
+
+        planes = [keep.tile([P, 2048], U8, name="planes%d" % s, align_bytes=64) for s in range(4)]
+        wh = [keep.tile([P, 2048], I32, name="wh%d" % g, align_bytes=64) for g in range(12)]
+        wo = [keep.tile([P, 2048], I32, name="wo%d" % g, align_bytes=64) for g in range(3)]
+        wo_last = [keep.tile([P, NCH], I32, name="wol%d" % c, align_bytes=64) for c in range(4)]
+        x_sb = keep.tile([P, C], BF16, name="x_sb")
+        ident = keep.tile([P, P], BF16, name="ident")
+        mix = keep.tile([P, 2, P], BF16, name="mix")
+
+        for s in range(4):
+            nc.vector.memset(planes[s][:].bitcast(I32), 0)
+        masks.make_identity(nc, ident[:])
+
+        nc.sync.dma_start(out=x_sb[:], in_=x_dram)
+        for s in range(4):
+            src = W_hidden_scales[4 * s : 4 * s + 4] if s < 3 else W_out_scales
+            for q in range(4):
+                nc.sync.dma_start(
+                    out=planes[s][32 * q : 32 * q + 16, :].bitcast(I32),
+                    in_=src[:, 4 * q : 4 * q + 4, :].bitcast(I32),
+                )
+        for g in range(12):
+            nc.sync.dma_start(out=wh[g][:], in_=W_hidden_words[g].rearrange("p n t -> p (n t)").bitcast(I32))
+        for g in range(3):
+            nc.sync.dma_start(out=wo[g][:], in_=W_out_words[g].rearrange("p n t -> p (n t)").bitcast(I32))
+        for c in range(4):
+            nc.sync.dma_start(
+                out=wo_last[c][:],
+                in_=W_out_words[3, :, c * NCH : (c + 1) * NCH, :].rearrange("p n t -> p (n t)").bitcast(I32),
+            )
+
+        ext = keep.tile([P, 2, 10, 10], BF16, name="ext")
+        idv = ident[:].rearrange("p (b i j) -> p b i j", b=2, i=8)
+        nc.vector.tensor_copy(out=ext[:, :, 1:9, 1:9], in_=idv)
+        nc.vector.tensor_copy(out=ext[:, :, 1:9, 0:1], in_=idv[:, :, :, 7:8])
+        nc.vector.tensor_copy(out=ext[:, :, 1:9, 9:10], in_=idv[:, :, :, 0:1])
+        nc.vector.tensor_copy(out=ext[:, :, 0:1, :], in_=ext[:, :, 8:9, :])
+        nc.vector.tensor_copy(out=ext[:, :, 9:10, :], in_=ext[:, :, 1:2, :])
+        dj = keep.tile([P, 2, 10, 8], BF16, name="dj")
+        di = keep.tile([P, 2, 8, 10], BF16, name="di")
+        sj = keep.tile([P, 2, 9, 8], BF16, name="sj")
+        si = keep.tile([P, 2, 8, 9], BF16, name="si")
+        nc.vector.tensor_tensor(out=dj[:], in0=ext[:, :, :, 2:10], in1=ext[:, :, :, 0:8], op=ALU.subtract)
+        nc.vector.tensor_tensor(out=di[:], in0=ext[:, :, 2:10, :], in1=ext[:, :, 0:8, :], op=ALU.subtract)
+        nc.vector.tensor_tensor(out=sj[:], in0=dj[:, :, 0:9, :], in1=dj[:, :, 1:10, :], op=ALU.add)
+        nc.vector.tensor_tensor(out=si[:], in0=di[:, :, :, 0:9], in1=di[:, :, :, 1:10], op=ALU.add)
+        nc.vector.tensor_tensor(
+            out=mix[:, 0, :].rearrange("p (b i j) -> p b i j", b=2, i=8),
+            in0=sj[:, :, 0:8, :], in1=sj[:, :, 1:9, :], op=ALU.add,
+        )
+        nc.vector.tensor_tensor(
+            out=mix[:, 1, :].rearrange("p (b i j) -> p b i j", b=2, i=8),
+            in0=si[:, :, :, 0:8], in1=si[:, :, :, 1:9], op=ALU.add,
+        )
+        moving = [mix[:, 0, :], mix[:, 1, :], ident[:]]
+
+        xs = [keep.tile([P, 4, P], BF16, name="xs%d" % gp) for gp in range(4)]
+        for gp in range(4):
+            nc.vector.tensor_copy(
+                out=xs[gp][:],
+                in_=x_sb[:, gp * 512 : (gp + 1) * 512].rearrange("m (p t) -> m t p", t=4),
+            )
+
+        grouped = [keep.tile([P, P, 4], BF16, name="grp%d" % g, align_bytes=64) for g in range(12)]
+        pcodes = [keep.tile([P, P], U32, name="pc%d" % g, align_bytes=64) for g in range(12)]
+        pscale = [keep.tile([P, P], U8, name="ps%d" % g, align_bytes=64) for g in range(12)]
+
+        def quantise(src, codes, scales):
+            nc.vector.quantize_mx(
+                out=codes[:].bitcast(FP8X4), scales=scales[:], in_=src[:].rearrange("p w t -> p (w t)")
+            )
+
+        turn = 0
+        for gp in range(4):
+            banks = [tp.tile([P, 4, P], F32, name="pt%d_%d" % (gp, s), tag="tp") for s in range(3)]
+            for t in range(4):
+                for s in range(3):
+                    nc.tensor.matmul(out=banks[s][:, t, :], lhsT=xs[gp][:, t, :], rhs=moving[s], start=True, stop=True)
+            for s in range(3):
+                view = banks[s][:].rearrange("p t w -> p w t")
+                if turn % 2 == 0:
+                    nc.scalar.copy(out=grouped[4 * s + gp][:], in_=view)
+                else:
+                    nc.vector.tensor_copy(out=grouped[4 * s + gp][:], in_=view)
+                turn += 1
+            if gp > 0:
+                for s in range(3):
+                    quantise(grouped[4 * s + gp - 1], pcodes[4 * s + gp - 1], pscale[4 * s + gp - 1])
+        for s in range(3):
+            quantise(grouped[4 * s + 3], pcodes[4 * s + 3], pscale[4 * s + 3])
+
+        hacc = [accp.tile([P, NCH], F32, name="hacc%d" % c, tag="acc") for c in range(4)]
+        for g in range(12):
+            for c in range(4):
+                cols = slice(c * NCH, (c + 1) * NCH)
+                nc.tensor.matmul_mx(
+                    out=hacc[c][:],
+                    lhsT=pcodes[g][:].bitcast(FP8X4),
+                    lhsT_scale=pscale[g][:],
+                    rhs=wh[g][:, cols].bitcast(FP8X4),
+                    rhs_scale=planes[g // 4][4 * (g % 4) : P, cols],
+                    start=(g == 0),
+                    stop=(g == 11),
+                )
+
+        hs = [keep.tile([P, 4, P], BF16, name="hs%d" % g) for g in range(4)]
+        hgrouped = [keep.tile([P, P, 4], BF16, name="hgrp%d" % g, align_bytes=64) for g in range(4)]
+        hcodes = [keep.tile([P, P], U32, name="hc%d" % g, align_bytes=64) for g in range(4)]
+        hscale = [keep.tile([P, P], U8, name="hsc%d" % g, align_bytes=64) for g in range(4)]
+        for g in range(4):
+            view = hacc[g][:].rearrange("m (p t) -> m t p", t=4)
+            if g % 2 == 0:
+                nc.vector.tensor_scalar_max(out=hs[g][:], in0=view, scalar1=0.0)
+            else:
+                nc.scalar.activation(out=hs[g][:], in_=view, func=ACT.Relu)
+        for g in range(4):
+            ht = tp.tile([P, 4, P], BF16, name="ht%d" % g, tag="tp")
+            for t in range(4):
+                nc.tensor.transpose(out=ht[:, t, :], in_=hs[g][:, t, :], identity=ident[:])
+            view = ht[:].rearrange("p t w -> p w t")
+            if g % 2 == 0:
+                nc.vector.tensor_copy(out=hgrouped[g][:], in_=view)
+            else:
+                nc.scalar.copy(out=hgrouped[g][:], in_=view)
+        for g in range(4):
+            quantise(hgrouped[g], hcodes[g], hscale[g])
+
+        oacc = [accp.tile([P, NCH], F32, name="oacc%d" % c, tag="acc") for c in range(4)]
+        res = [keep.tile([P, NCH], F32, name="res%d" % c) for c in range(4)]
+        for g in range(4):
+            for c in range(4):
+                cols = slice(c * NCH, (c + 1) * NCH)
+                nc.tensor.matmul_mx(
+                    out=oacc[c][:],
+                    lhsT=hcodes[g][:].bitcast(FP8X4),
+                    lhsT_scale=hscale[g][:],
+                    rhs=(wo[g][:, cols] if g < 3 else wo_last[c][:]).bitcast(FP8X4),
+                    rhs_scale=planes[3][4 * g : P, cols],
+                    start=(g == 0),
+                    stop=(g == 3),
+                )
+                if g == 3:
+                    if c % 2 == 0:
+                        nc.vector.tensor_copy(out=res[c][:], in_=oacc[c][:])
+                    else:
+                        nc.scalar.copy(out=res[c][:], in_=oacc[c][:])
+                    nc.sync.dma_start(out=out_dram[:, cols], in_=res[c][:])

@@ -45,9 +45,9 @@ def tile_nn_w_kernel(tc, state_grid, W_hidden_words, W_hidden_scales, W_out_word
         for s in range(4):
             src = W_hidden_scales[4 * s : 4 * s + 4] if s < 3 else W_out_scales
             for q in range(4):
-                nc.sync.dma_start(
-                    out=planes[s][32 * q : 32 * q + 16, :].bitcast(I32),
-                    in_=src[:, 4 * q : 4 * q + 4, :].bitcast(I32),
+                nc.gpsimd.dma_start(
+                    out=planes[s][32 * q : 32 * q + 16, :].bitcast(F32),
+                    in_=src[:, 4 * q : 4 * q + 4, :].bitcast(F32),
                 )
         for g in range(12):
             nc.sync.dma_start(out=wh[g][:], in_=W_hidden_words[g].rearrange("p n t -> p (n t)").bitcast(I32))

@@ -16,6 +16,7 @@ P = 128
 C = 2048
 HIDDEN = 2048
 NCH = 512
+TAIL = ((0, 1024), (1024, 512), (1536, 256), (1792, 256))
 FLOPS = 2 * P * (3 * C) * HIDDEN + 2 * P * HIDDEN * C
 
 
@@ -31,8 +32,8 @@ def tile_nn_w_kernel(tc, state_grid, W_hidden_words, W_hidden_scales, W_out_word
 
         planes = [keep.tile([P, 2048], U8, name="planes%d" % s, align_bytes=64) for s in range(4)]
         wh = [keep.tile([P, 2048], I32, name="wh%d" % g, align_bytes=64) for g in range(12)]
-        wo = [keep.tile([P, 2048], I32, name="wo%d" % g, align_bytes=64) for g in range(3)]
-        wo_last = [keep.tile([P, NCH], I32, name="wol%d" % c, align_bytes=64) for c in range(4)]
+        wo = [keep.tile([P, 2048], I32, name="wo%d" % g, align_bytes=64) for g in range(2)]
+        wo_tail = [keep.tile([P, 2, n], I32, name="wot%d" % i, align_bytes=64) for i, (c, n) in enumerate(TAIL)]
         x_sb = keep.tile([P, C], BF16, name="x_sb")
         ident = keep.tile([P, P], BF16, name="ident")
         mix = keep.tile([P, 2, P], BF16, name="mix")
@@ -51,12 +52,12 @@ def tile_nn_w_kernel(tc, state_grid, W_hidden_words, W_hidden_scales, W_out_word
                 )
         for g in range(12):
             nc.sync.dma_start(out=wh[g][:], in_=W_hidden_words[g].rearrange("p n t -> p (n t)").bitcast(I32))
-        for g in range(3):
+        for g in range(2):
             nc.sync.dma_start(out=wo[g][:], in_=W_out_words[g].rearrange("p n t -> p (n t)").bitcast(I32))
-        for c in range(4):
+        for i, (c, n) in enumerate(TAIL):
             nc.sync.dma_start(
-                out=wo_last[c][:],
-                in_=W_out_words[3, :, c * NCH : (c + 1) * NCH, :].rearrange("p n t -> p (n t)").bitcast(I32),
+                out=wo_tail[i][:],
+                in_=W_out_words[2:4, :, c : c + n, :].rearrange("g p n t -> p g (n t)").bitcast(I32),
             )
 
         ext = keep.tile([P, 2, 10, 10], BF16, name="ext")
@@ -155,23 +156,37 @@ def tile_nn_w_kernel(tc, state_grid, W_hidden_words, W_hidden_scales, W_out_word
         for g in range(4):
             quantise(hgrouped[g], hcodes[g], hscale[g])
 
-        oacc = [accp.tile([P, NCH], F32, name="oacc%d" % c, tag="acc") for c in range(4)]
-        res = [keep.tile([P, NCH], F32, name="res%d" % c) for c in range(4)]
-        for g in range(4):
-            for c in range(4):
-                cols = slice(c * NCH, (c + 1) * NCH)
-                nc.tensor.matmul_mx(
-                    out=oacc[c][:],
-                    lhsT=hcodes[g][:].bitcast(FP8X4),
-                    lhsT_scale=hscale[g][:],
-                    rhs=(wo[g][:, cols] if g < 3 else wo_last[c][:]).bitcast(FP8X4),
-                    rhs_scale=planes[3][4 * g : P, cols],
-                    start=(g == 0),
-                    stop=(g == 3),
-                )
-                if g == 3:
-                    if c % 2 == 0:
-                        nc.vector.tensor_copy(out=res[c][:], in_=oacc[c][:])
-                    else:
-                        nc.scalar.copy(out=res[c][:], in_=oacc[c][:])
-                    nc.sync.dma_start(out=out_dram[:, cols], in_=res[c][:])
+        pieces = [(0, 0, 0, 512), (0, 512, 512, 512), (1, 0, 1024, 512), (2, 0, 1536, 256), (3, 0, 1792, 256)]
+        oacc = []
+        res = []
+        for i, (tail, tc0, c0, n) in enumerate(pieces):
+            if i < 3:
+                oacc.append(accp.tile([P, n], F32, name="oacc%d" % i, tag="acc"))
+            else:
+                oacc.append(tp.tile([P, n], F32, name="oacc%d" % i, tag="tp"))
+            res.append(keep.tile([P, n], F32, name="res%d" % i))
+
+        def multiply(i, g):
+            tail, tc0, c0, n = pieces[i]
+            codes = wo[g][:, c0 : c0 + n] if g < 2 else wo_tail[tail][:, g - 2, tc0 : tc0 + n]
+            nc.tensor.matmul_mx(
+                out=oacc[i][:],
+                lhsT=hcodes[g][:].bitcast(FP8X4),
+                lhsT_scale=hscale[g][:],
+                rhs=codes.bitcast(FP8X4),
+                rhs_scale=planes[3][4 * g : P, c0 : c0 + n],
+                start=(g == 0),
+                stop=(g == 3),
+            )
+
+        for g in range(2):
+            for i in range(5):
+                multiply(i, g)
+        for i, (tail, tc0, c0, n) in enumerate(pieces):
+            multiply(i, 2)
+            multiply(i, 3)
+            if i % 2 == 0:
+                nc.vector.tensor_copy(out=res[i][:], in_=oacc[i][:])
+            else:
+                nc.scalar.copy(out=res[i][:], in_=oacc[i][:])
+            nc.sync.dma_start(out=out_dram[:, c0 : c0 + n], in_=res[i][:])

from contextlib import ExitStack

import concourse.masks as masks
import concourse.mybir as mybir

F32 = mybir.dt.float32
BF16 = mybir.dt.bfloat16
I32 = mybir.dt.int32
U32 = mybir.dt.uint32
U8 = mybir.dt.uint8
FP8X4 = mybir.dt.float8_e4m3fn_x4
ALU = mybir.AluOpType
ACT = mybir.ActivationFunctionType

P = 128
C = 2048
HIDDEN = 2048
NCH = 512
TAIL = ((0, 1024), (1024, 512), (1536, 256), (1792, 256))
FLOPS = 2 * P * (3 * C) * HIDDEN + 2 * P * HIDDEN * C


def tile_nn_w_kernel(tc, state_grid, W_hidden_words, W_hidden_scales, W_out_words, W_out_scales, out):
    nc = tc.nc
    x_dram = state_grid.flatten_outer_dims()
    out_dram = out.flatten_outer_dims()
    with ExitStack() as ctx:
        keep = ctx.enter_context(tc.tile_pool(name="keep", bufs=1))
        tp = ctx.enter_context(tc.psum_pool(name="tp", bufs=4))
        accp = ctx.enter_context(tc.psum_pool(name="accp", bufs=4))
        ctx.enter_context(tc.manual_schedule())

        planes = [keep.tile([P, 2048], U8, name="planes%d" % s, align_bytes=64) for s in range(4)]
        wh = [keep.tile([P, 2048], I32, name="wh%d" % g, align_bytes=64) for g in range(12)]
        wo = [keep.tile([P, 2048], I32, name="wo%d" % g, align_bytes=64) for g in range(2)]
        wo_tail = [keep.tile([P, 2, n], I32, name="wot%d" % i, align_bytes=64) for i, (c, n) in enumerate(TAIL)]
        x_sb = keep.tile([P, C], BF16, name="x_sb")
        ident = keep.tile([P, P], BF16, name="ident")
        mix = keep.tile([P, 2, P], BF16, name="mix")

        for s in range(4):
            nc.vector.memset(planes[s][:].bitcast(I32), 0)
        masks.make_identity(nc, ident[:])

        nc.sync.dma_start(out=x_sb[:], in_=x_dram)
        for s in range(4):
            src = W_hidden_scales[4 * s : 4 * s + 4] if s < 3 else W_out_scales
            for q in range(4):
                nc.gpsimd.dma_start(
                    out=planes[s][32 * q : 32 * q + 16, :].bitcast(F32),
                    in_=src[:, 4 * q : 4 * q + 4, :].bitcast(F32),
                )
        for g in range(12):
            nc.sync.dma_start(out=wh[g][:], in_=W_hidden_words[g].rearrange("p n t -> p (n t)").bitcast(I32))
        for g in range(2):
            nc.sync.dma_start(out=wo[g][:], in_=W_out_words[g].rearrange("p n t -> p (n t)").bitcast(I32))
        for i, (c, n) in enumerate(TAIL):
            nc.sync.dma_start(
                out=wo_tail[i][:],
                in_=W_out_words[2:4, :, c : c + n, :].rearrange("g p n t -> p g (n t)").bitcast(I32),
            )

        ext = keep.tile([P, 2, 10, 10], BF16, name="ext")
        idv = ident[:].rearrange("p (b i j) -> p b i j", b=2, i=8)
        nc.vector.tensor_copy(out=ext[:, :, 1:9, 1:9], in_=idv)
        nc.vector.tensor_copy(out=ext[:, :, 1:9, 0:1], in_=idv[:, :, :, 7:8])
        nc.vector.tensor_copy(out=ext[:, :, 1:9, 9:10], in_=idv[:, :, :, 0:1])
        nc.vector.tensor_copy(out=ext[:, :, 0:1, :], in_=ext[:, :, 8:9, :])
        nc.vector.tensor_copy(out=ext[:, :, 9:10, :], in_=ext[:, :, 1:2, :])
        dj = keep.tile([P, 2, 10, 8], BF16, name="dj")
        di = keep.tile([P, 2, 8, 10], BF16, name="di")
        sj = keep.tile([P, 2, 9, 8], BF16, name="sj")
        si = keep.tile([P, 2, 8, 9], BF16, name="si")
        nc.vector.tensor_tensor(out=dj[:], in0=ext[:, :, :, 2:10], in1=ext[:, :, :, 0:8], op=ALU.subtract)
        nc.vector.tensor_tensor(out=di[:], in0=ext[:, :, 2:10, :], in1=ext[:, :, 0:8, :], op=ALU.subtract)
        nc.vector.tensor_tensor(out=sj[:], in0=dj[:, :, 0:9, :], in1=dj[:, :, 1:10, :], op=ALU.add)
        nc.vector.tensor_tensor(out=si[:], in0=di[:, :, :, 0:9], in1=di[:, :, :, 1:10], op=ALU.add)
        nc.vector.tensor_tensor(
            out=mix[:, 0, :].rearrange("p (b i j) -> p b i j", b=2, i=8),
            in0=sj[:, :, 0:8, :], in1=sj[:, :, 1:9, :], op=ALU.add,
        )
        nc.vector.tensor_tensor(
            out=mix[:, 1, :].rearrange("p (b i j) -> p b i j", b=2, i=8),
            in0=si[:, :, :, 0:8], in1=si[:, :, :, 1:9], op=ALU.add,
        )
        moving = [mix[:, 0, :], mix[:, 1, :], ident[:]]

        xs = [keep.tile([P, 4, P], BF16, name="xs%d" % gp) for gp in range(4)]
        for gp in range(4):
            nc.vector.tensor_copy(
                out=xs[gp][:],
                in_=x_sb[:, gp * 512 : (gp + 1) * 512].rearrange("m (p t) -> m t p", t=4),
            )

        grouped = [keep.tile([P, P, 4], BF16, name="grp%d" % g, align_bytes=64) for g in range(12)]
        pcodes = [keep.tile([P, P], U32, name="pc%d" % g, align_bytes=64) for g in range(12)]
        pscale = [keep.tile([P, P], U8, name="ps%d" % g, align_bytes=64) for g in range(12)]

        def quantise(src, codes, scales):
            nc.vector.quantize_mx(
                out=codes[:].bitcast(FP8X4), scales=scales[:], in_=src[:].rearrange("p w t -> p (w t)")
            )

        turn = 0
        for gp in range(4):
            banks = [tp.tile([P, 4, P], F32, name="pt%d_%d" % (gp, s), tag="tp") for s in range(3)]
            for t in range(4):
                for s in range(3):
                    nc.tensor.matmul(out=banks[s][:, t, :], lhsT=xs[gp][:, t, :], rhs=moving[s], start=True, stop=True)
            for s in range(3):
                view = banks[s][:].rearrange("p t w -> p w t")
                if turn % 2 == 0:
                    nc.scalar.copy(out=grouped[4 * s + gp][:], in_=view)
                else:
                    nc.vector.tensor_copy(out=grouped[4 * s + gp][:], in_=view)
                turn += 1
            if gp > 0:
                for s in range(3):
                    quantise(grouped[4 * s + gp - 1], pcodes[4 * s + gp - 1], pscale[4 * s + gp - 1])
        for s in range(3):
            quantise(grouped[4 * s + 3], pcodes[4 * s + 3], pscale[4 * s + 3])

        hacc = [accp.tile([P, NCH], F32, name="hacc%d" % c, tag="acc") for c in range(4)]
        for g in range(12):
            for c in range(4):
                cols = slice(c * NCH, (c + 1) * NCH)
                nc.tensor.matmul_mx(
                    out=hacc[c][:],
                    lhsT=pcodes[g][:].bitcast(FP8X4),
                    lhsT_scale=pscale[g][:],
                    rhs=wh[g][:, cols].bitcast(FP8X4),
                    rhs_scale=planes[g // 4][4 * (g % 4) : P, cols],
                    start=(g == 0),
                    stop=(g == 11),
                )

        hs = [keep.tile([P, 4, P], BF16, name="hs%d" % g) for g in range(4)]
        hgrouped = [keep.tile([P, P, 4], BF16, name="hgrp%d" % g, align_bytes=64) for g in range(4)]
        hcodes = [keep.tile([P, P], U32, name="hc%d" % g, align_bytes=64) for g in range(4)]
        hscale = [keep.tile([P, P], U8, name="hsc%d" % g, align_bytes=64) for g in range(4)]
        for g in range(4):
            view = hacc[g][:].rearrange("m (p t) -> m t p", t=4)
            if g % 2 == 0:
                nc.vector.tensor_scalar_max(out=hs[g][:], in0=view, scalar1=0.0)
            else:
                nc.scalar.activation(out=hs[g][:], in_=view, func=ACT.Relu)
        for g in range(4):
            ht = tp.tile([P, 4, P], BF16, name="ht%d" % g, tag="tp")
            for t in range(4):
                nc.tensor.transpose(out=ht[:, t, :], in_=hs[g][:, t, :], identity=ident[:])
            view = ht[:].rearrange("p t w -> p w t")
            if g % 2 == 0:
                nc.vector.tensor_copy(out=hgrouped[g][:], in_=view)
            else:
                nc.scalar.copy(out=hgrouped[g][:], in_=view)
        for g in range(4):
            quantise(hgrouped[g], hcodes[g], hscale[g])

        pieces = [(0, 0, 0, 512), (0, 512, 512, 512), (1, 0, 1024, 512), (2, 0, 1536, 256), (3, 0, 1792, 256)]
        oacc = []
        res = []
        for i, (tail, tc0, c0, n) in enumerate(pieces):
            if i < 3:
                oacc.append(accp.tile([P, n], F32, name="oacc%d" % i, tag="acc"))
            else:
                oacc.append(tp.tile([P, n], F32, name="oacc%d" % i, tag="tp"))
            res.append(keep.tile([P, n], F32, name="res%d" % i))

        def multiply(i, g):
            tail, tc0, c0, n = pieces[i]
            codes = wo[g][:, c0 : c0 + n] if g < 2 else wo_tail[tail][:, g - 2, tc0 : tc0 + n]
            nc.tensor.matmul_mx(
                out=oacc[i][:],
                lhsT=hcodes[g][:].bitcast(FP8X4),
                lhsT_scale=hscale[g][:],
                rhs=codes.bitcast(FP8X4),
                rhs_scale=planes[3][4 * g : P, c0 : c0 + n],
                start=(g == 0),
                stop=(g == 3),
            )

        for g in range(2):
            for i in range(5):
                multiply(i, g)
        for i, (tail, tc0, c0, n) in enumerate(pieces):
            multiply(i, 2)
            multiply(i, 3)
            if i % 2 == 0:
                nc.vector.tensor_copy(out=res[i][:], in_=oacc[i][:])
            else:
                nc.scalar.copy(out=res[i][:], in_=oacc[i][:])
            nc.sync.dma_start(out=out_dram[:, c0 : c0 + n], in_=res[i][:])
